import numpy as np
import ml_dtypes


def mxq(x, axis, fmt="e4m3"):
    dtype, down = {"e4m3": (ml_dtypes.float8_e4m3fn, 7), "e5m2": (ml_dtypes.float8_e5m2, 14)}[fmt]
    v = np.moveaxis(np.asarray(x, np.float32).astype(ml_dtypes.bfloat16).astype(np.float64), axis, -1)
    blocks = v.reshape(v.shape[:-1] + (-1, 32))
    amax = np.abs(blocks).max(-1, keepdims=True)
    byte = np.maximum(np.where(amax > 0, np.frexp(amax)[1] - 1 + 127, 0) - down, 1)
    scale = np.exp2(byte - 127.0)
    codes = (blocks / scale).astype(np.float32).astype(dtype).astype(np.float64)
    return np.moveaxis((codes * scale).reshape(v.shape), -1, axis)


WIDE = False


def mx_kscale(k):
    if not WIDE:
        return np.ones(k)
    levels = np.array([10, -10, 5, -5, 0])
    a = np.random.permutation(np.resize(levels, k // 512 * 4)).reshape(k // 512, 4)
    idx = np.arange(k)
    return np.exp2(a[idx // 512, idx % 128 // 32])


BF16 = ml_dtypes.bfloat16


def bf(x):
    return np.asarray(x, np.float32).astype(BF16)


def f64(x):
    return np.asarray(x).astype(np.float64)


E2M1 = np.array([0.0, 0.5, 1.0, 1.5, 2.0, 3.0, 4.0, 6.0, -0.0, -0.5, -1.0, -1.5, -2.0, -3.0, -4.0, -6.0])


def pack_weight(w, fmt):
    k, n = w.shape
    w = f64(bf(w)).reshape(k // 32, 32, n)
    amax = np.abs(w).max(1)
    if fmt == "e4m3":
        byte = np.frexp(amax)[1] - 1 + 127 - 7
    else:
        mant, ex = np.frexp(amax / 6.0)
        byte = np.where(mant > 0.5, ex, ex - 1) + 127
    byte = np.clip(np.where(amax > 0, byte, 1), 1, 254)
    scaled = (w * np.exp2(127.0 - byte)[:, None, :]).reshape(k, n).astype(np.float32)
    by_word = np.ascontiguousarray(scaled.reshape(k // 512, 128, 4, n).transpose(0, 1, 3, 2))
    if fmt == "e4m3":
        words = by_word.astype(ml_dtypes.float8_e4m3fn).view(np.uint8)
    else:
        c = by_word.astype(ml_dtypes.float4_e2m1fn).view(np.uint8) & 0xF
        words = c[..., 0::2] | (c[..., 1::2] << 4)
    return np.ascontiguousarray(words), np.ascontiguousarray(byte.astype(np.uint8).reshape(k // 512, 16, n))


def unpack_weight(words, scales, fmt):
    g, p, n, _ = words.shape
    if fmt == "e4m3":
        vals = np.ascontiguousarray(words).view(ml_dtypes.float8_e4m3fn).astype(np.float64)
    else:
        nib = np.empty((g, p, n, 4), np.uint8)
        nib[..., 0::2] = words & 0xF
        nib[..., 1::2] = words >> 4
        vals = E2M1[nib]
    vals = vals * np.repeat(np.exp2(scales.astype(np.float64) - 127.0), 8, axis=1)[..., None]
    return vals.transpose(0, 1, 3, 2).reshape(g * 512, n)


E, F, H, MID, OUT = 16384, 64, 192, 512, 128
D = 2 * (F + H)
IN = D + 1
FMT = "e4m3"


def setup_inputs():
    s = mx_kscale(D)
    t = mx_kscale(MID)
    w1 = np.concatenate([np.random.standard_normal((MID, D)) / np.sqrt(D) / s[None, :],
                         np.random.standard_normal((MID, 1)) * 0.5], axis=1) * t[:, None]
    dst_node_feat = bf(np.random.standard_normal((E, F)) * s[:F])
    dst_node_hidden = bf(np.random.standard_normal((E, H)) * s[F:F + H])
    src_node_feat = bf(np.random.standard_normal((E, F)) * s[F + H:2 * F + H])
    src_node_hidden = bf(np.random.standard_normal((E, H)) * s[2 * F + H:])
    edge_feat = bf(np.random.standard_normal(E))
    b1 = bf(np.random.standard_normal(MID) * 0.3 * t)
    w2 = np.random.standard_normal((OUT, MID)) / np.sqrt(MID) / t[None, :]
    w2_words, w2_scales = pack_weight(np.ascontiguousarray(w2.T), FMT)
    b2 = bf(np.random.standard_normal(OUT) * 0.3)
    return {"dst_node_feat": dst_node_feat,
            "dst_node_hidden": dst_node_hidden,
            "src_node_feat": src_node_feat,
            "src_node_hidden": src_node_hidden,
            "edge_feat": edge_feat,
            "W1": bf(w1),
            "b1": b1,
            "W2_words": w2_words,
            "W2_scales": w2_scales,
            "b2": b2}


def reference(dst_node_feat, dst_node_hidden, src_node_feat, src_node_hidden, edge_feat, W1, b1, W2_words, W2_scales, b2):
    x = np.concatenate([f64(dst_node_feat), f64(dst_node_hidden), f64(src_node_feat), f64(src_node_hidden),
                        f64(edge_feat)[:, None]], axis=1)
    w1 = f64(W1)
    pre = (mxq(x[:, :D], 1, "e4m3") @ mxq(w1[:, :D], 1, "e4m3").T) + x[:, D:] * w1[:, D] + f64(b1)
    h = np.maximum(pre, 0.0)
    return np.tanh((mxq(h, 1, "e4m3") @ unpack_weight(W2_words, W2_scales, FMT)) + f64(b2))

@@ -1,0 +1,267 @@
+from contextlib import ExitStack
+
+import concourse.mybir as mybir
+from concourse.masks import make_identity
+
+F32 = mybir.dt.float32
+BF16 = mybir.dt.bfloat16
+U32 = mybir.dt.uint32
+U8 = mybir.dt.uint8
+I32 = mybir.dt.int32
+FP8X4 = mybir.dt.float8_e4m3fn_x4
+ALU = mybir.AluOpType
+ACT = mybir.ActivationFunctionType
+
+P = 128
+PACK = 4
+E, F, H, MID, OUT = 16384, 64, 192, 512, 128
+NODE = 2 * (F + H)
+NODE_WORDS = NODE // 2
+
+TILES_PER_GROUP = 4
+TILES_PER_CHUNK = 8
+GROUPS_PER_CHUNK = TILES_PER_CHUNK // TILES_PER_GROUP
+N_CHUNKS = E // (P * TILES_PER_CHUNK)
+N_GROUPS = N_CHUNKS * GROUPS_PER_CHUNK
+CHUNKS_AHEAD = 3
+EDGE_TERM_AHEAD = 4
+
+FLOPS = 2 * E * ((NODE + 1) * MID + MID * OUT)
+
+
+def tile_edgenetwork_kernel(
+    tc,
+    dst_node_feat,
+    dst_node_hidden,
+    src_node_feat,
+    src_node_hidden,
+    edge_feat,
+    W1,
+    b1,
+    W2_words,
+    W2_scales,
+    b2,
+    out,
+):
+    nc = tc.nc
+
+    def by_chunk(rows):
+        return rows.rearrange("(q c i) f -> q c i f", c=P, i=TILES_PER_CHUNK)
+
+    node_inputs = (
+        (by_chunk(dst_node_feat), 0, F),
+        (by_chunk(dst_node_hidden), F, H),
+        (by_chunk(src_node_feat), F + H, F),
+        (by_chunk(src_node_hidden), 2 * F + H, H),
+    )
+    out_by_chunk = by_chunk(out)
+
+    with ExitStack() as stack:
+        const = stack.enter_context(tc.tile_pool(name="const", bufs=1))
+        work = stack.enter_context(tc.tile_pool(name="work", bufs=2))
+        psum = stack.enter_context(tc.psum_pool(name="psum", bufs=1))
+        stack.enter_context(tc.manual_schedule())
+
+        x_chunks = {}
+
+        def load_chunk(q):
+            x_sb = work.tile([P, TILES_PER_CHUNK, NODE], BF16, tag="x", bufs=CHUNKS_AHEAD + 1, name="x_sb")
+            for rows, first, width in node_inputs:
+                nc.sync.dma_start(out=x_sb[:, :, first : first + width], in_=rows[q])
+            x_chunks[q] = x_sb
+
+        w1_rows = const.tile([P, PACK, NODE + 1], BF16)
+        nc.sync.dma_start(out=w1_rows[:], in_=W1.rearrange("(j t) k -> j t k", t=PACK))
+        load_chunk(0)
+        edge_cols = const.tile([P, N_CHUNKS * TILES_PER_CHUNK], BF16)
+        nc.scalar.dma_start(
+            out=edge_cols[:].rearrange("c (q i) -> c q i", i=TILES_PER_CHUNK),
+            in_=edge_feat.rearrange("(q c i) -> c q i", c=P, i=TILES_PER_CHUNK),
+        )
+        b1_bf = const.tile([P, PACK], BF16)
+        nc.scalar.dma_start(out=b1_bf[:], in_=b1.rearrange("(p t) -> p t", t=PACK))
+        b2_bf = const.tile([P, OUT], BF16)
+        nc.scalar.dma_start(out=b2_bf[:], in_=b2.partition_broadcast(P))
+        load_chunk(1)
+
+        w2_codes = const.tile([P, OUT * PACK], U8, align_bytes=64)
+        nc.sync.dma_start(
+            out=w2_codes[:].bitcast(I32),
+            in_=W2_words.rearrange("g p n t -> (g p) (n t)").bitcast(I32),
+        )
+        w2_scales = const.tile([P, OUT], U8, align_bytes=64)
+        nc.vector.memset(w2_scales[:].bitcast(I32), 0)
+        for quadrant in range(4):
+            nc.sync.dma_start(
+                out=w2_scales[32 * quadrant : 32 * quadrant + 4, :].bitcast(I32),
+                in_=W2_scales[0, 4 * quadrant : 4 * quadrant + 4, :].bitcast(I32),
+            )
+        load_chunk(2)
+
+        ident_f32 = const.tile([P, P], F32)
+        make_identity(nc, ident_f32[:])
+        ident_bf = const.tile([P, P], BF16)
+        make_identity(nc, ident_bf[:])
+
+        w1_nodes = const.tile([P, PACK, NODE], BF16)
+        nc.vector.tensor_copy(out=w1_nodes[:], in_=w1_rows[:, :, 0:NODE])
+        w1_edge = const.tile([P, PACK], F32)
+        nc.vector.tensor_copy(out=w1_edge[:], in_=w1_rows[:, :, NODE])
+        b1_f32 = const.tile([P, PACK], F32)
+        nc.vector.tensor_copy(out=b1_f32[:], in_=b1_bf[:])
+        b2_f32 = const.tile([P, OUT], F32)
+        nc.vector.tensor_copy(out=b2_f32[:], in_=b2_bf[:])
+
+        def rows_to_grouped(row_tiles):
+            grouped = work.tile([P, TILES_PER_GROUP * P * PACK], BF16, tag="grouped", align_bytes=64, name="grouped")
+            grouped_words = grouped[:].bitcast(F32)
+            for pair in range(2):
+                xt = psum.tile([P, 4, P], F32, tag="xt", bufs=2, name="xt")
+                for i in range(2):
+                    words = row_tiles[2 * pair + i].bitcast(F32)
+                    for u in range(2):
+                        nc.tensor.transpose(xt[:, 2 * i + u, :], words[:, P * u : P * (u + 1)], ident_f32[:])
+                nc.scalar.copy(
+                    out=grouped_words[:, 512 * pair : 512 * (pair + 1)].rearrange(
+                        "p (i c u) -> p i c u", i=2, u=2
+                    ),
+                    in_=xt[:].rearrange("p (i u) c -> p i c u", u=2),
+                )
+            return grouped
+
+        def quantise(grouped, codes, scales):
+            nc.vector.quantize_mx(out=codes.bitcast(FP8X4), scales=scales, in_=grouped)
+
+        w1_codes = const.tile([P, PACK * P], U32, align_bytes=64)
+        w1_scales = const.tile([P, PACK * P], U8, align_bytes=64)
+        w1_grouped = rows_to_grouped([w1_nodes[:, t, :] for t in range(PACK)])
+        quantise(w1_grouped[:], w1_codes[:], w1_scales[:])
+
+        edge_terms = {}
+
+        def prepare_edge_term(q):
+            spread = psum.tile([P, TILES_PER_CHUNK, P], BF16, tag="spread", name="spread")
+            for i in range(TILES_PER_CHUNK):
+                m = TILES_PER_CHUNK * q + i
+                nc.tensor.transpose(spread[:, i, :], edge_cols[:, m : m + 1].to_broadcast([P, P]), ident_bf[:])
+            edge_all = work.tile([P, TILES_PER_CHUNK, P], BF16, tag="edge_all", name="edge_all")
+            nc.scalar.copy(out=edge_all[:], in_=spread[:])
+            edge_term = work.tile([P, PACK, TILES_PER_CHUNK, P], F32, tag="edge_term", bufs=3, name="edge_term")
+            for t in range(PACK):
+                nc.gpsimd.tensor_scalar(
+                    out=edge_term[:, t, :, :],
+                    in0=edge_all[:],
+                    scalar1=w1_edge[:, t : t + 1],
+                    scalar2=b1_f32[:, t : t + 1],
+                    op0=ALU.mult,
+                    op1=ALU.add,
+                )
+            edge_terms[q] = edge_term
+
+        x_grouped = {}
+        x_codes = {}
+        x_scales = {}
+        sums1 = {}
+        h_grouped = {}
+        h_codes = {}
+        h_scales = {}
+        sums2 = {}
+
+        def transpose_x(g):
+            q, half = divmod(g, GROUPS_PER_CHUNK)
+            x_sb = x_chunks[q]
+            x_grouped[g] = rows_to_grouped(
+                [x_sb[:, TILES_PER_GROUP * half + j, :] for j in range(TILES_PER_GROUP)]
+            )
+
+        def quantise_x(g):
+            x_codes[g] = work.tile([P, TILES_PER_GROUP * P], U32, tag="x_codes", align_bytes=64, name="x_codes")
+            x_scales[g] = work.tile([P, TILES_PER_GROUP * P], U8, tag="x_scales", align_bytes=64, name="x_scales")
+            quantise(x_grouped[g][:], x_codes[g][:], x_scales[g][:])
+
+        def layer1(g, j):
+            sums = psum.tile([P, PACK, P], F32, tag="sums1", bufs=4, name="sums")
+            cols = slice(P * j, P * (j + 1))
+            for t in range(PACK):
+                block = slice(P * t, P * (t + 1))
+                nc.tensor.matmul_mx(
+                    out=sums[:, t, :],
+                    lhsT=w1_codes[:, block].bitcast(FP8X4),
+                    lhsT_scale=w1_scales[:, block],
+                    rhs=x_codes[g][:, cols].bitcast(FP8X4),
+                    rhs_scale=x_scales[g][:, cols],
+                    start=True,
+                    stop=True,
+                )
+            sums1[(g, j)] = sums
+
+        def hidden(g, j):
+            q, half = divmod(g, GROUPS_PER_CHUNK)
+            if j == 0:
+                h_grouped[g] = work.tile([P, TILES_PER_GROUP, P * PACK], BF16, tag="h", bufs=3, align_bytes=64, name="h")
+            pre = work.tile([P, P, PACK], BF16, tag="pre", bufs=3, name="pre")
+            nc.vector.tensor_tensor(
+                out=pre[:],
+                in0=sums1[(g, j)][:].rearrange("p t c -> p c t"),
+                in1=edge_terms[q][:, :, TILES_PER_GROUP * half + j, :].rearrange("p t c -> p c t"),
+                op=ALU.add,
+            )
+            nc.scalar.activation(
+                out=h_grouped[g][:, j, :], in_=pre[:].rearrange("p c t -> p (c t)"), func=ACT.Relu
+            )
+
+        def quantise_h(g):
+            h_codes[g] = work.tile([P, TILES_PER_GROUP * P], U32, tag="h_codes", align_bytes=64, name="h_codes")
+            h_scales[g] = work.tile([P, TILES_PER_GROUP * P], U8, tag="h_scales", align_bytes=64, name="h_scales")
+            quantise(h_grouped[g][:].rearrange("p j w -> p (j w)"), h_codes[g][:], h_scales[g][:])
+
+        def layer2(g):
+            sums = psum.tile([P, TILES_PER_GROUP, OUT], F32, tag="sums2", name="sums")
+            for j in range(TILES_PER_GROUP):
+                cols = slice(P * j, P * (j + 1))
+                nc.tensor.matmul_mx(
+                    out=sums[:, j, :],
+                    lhsT=h_codes[g][:, cols].bitcast(FP8X4),
+                    lhsT_scale=h_scales[g][:, cols],
+                    rhs=w2_codes[:].bitcast(FP8X4),
+                    rhs_scale=w2_scales[:],
+                    start=True,
+                    stop=True,
+                )
+            sums2[g] = sums
+
+        def finish(g):
+            q, half = divmod(g, GROUPS_PER_CHUNK)
+            biased = work.tile([P, TILES_PER_GROUP, OUT], F32, tag="biased", name="biased")
+            nc.vector.tensor_tensor(
+                out=biased[:],
+                in0=sums2[g][:],
+                in1=b2_f32[:].unsqueeze(1).to_broadcast([P, TILES_PER_GROUP, OUT]),
+                op=ALU.add,
+            )
+            result = work.tile([P, TILES_PER_GROUP, OUT], F32, tag="result", bufs=3, name="result")
+            nc.scalar.activation(out=result[:], in_=biased[:], func=ACT.Tanh)
+            first = TILES_PER_GROUP * half
+            nc.sync.dma_start(out=out_by_chunk[q][:, first : first + TILES_PER_GROUP, :], in_=result[:])
+
+        prepare_edge_term(0)
+        for g in range(-2, N_GROUPS + 2):
+            if 0 <= g + 2 < N_GROUPS:
+                if (g + 2) % GROUPS_PER_CHUNK == 0 and (g + 2) // GROUPS_PER_CHUNK + CHUNKS_AHEAD < N_CHUNKS:
+                    load_chunk((g + 2) // GROUPS_PER_CHUNK + CHUNKS_AHEAD)
+                transpose_x(g + 2)
+            ahead = g + EDGE_TERM_AHEAD
+            if ahead % GROUPS_PER_CHUNK == 0 and 0 < ahead < N_GROUPS:
+                prepare_edge_term(ahead // GROUPS_PER_CHUNK)
+            if 0 <= g + 1 < N_GROUPS:
+                quantise_x(g + 1)
+            if 0 <= g - 2 < N_GROUPS:
+                finish(g - 2)
+            if 0 <= g - 1 < N_GROUPS:
+                quantise_h(g - 1)
+                layer2(g - 1)
+            for j in range(TILES_PER_GROUP):
+                if 0 <= g < N_GROUPS:
+                    hidden(g, j)
+                if 0 <= g + 1 < N_GROUPS:
+                    layer1(g + 1, j)

@@ -112,40 +112,52 @@ def tile_edgenetwork_kernel(
         b2_f32 = const.tile([P, OUT], F32)
         nc.vector.tensor_copy(out=b2_f32[:], in_=b2_bf[:])
 
-        def rows_to_grouped(row_tiles):
-            grouped = work.tile([P, TILES_PER_GROUP * P * PACK], BF16, tag="grouped", align_bytes=64, name="grouped")
-            grouped_words = grouped[:].bitcast(F32)
+        def transpose_rows(row_tiles):
+            banks = []
             for pair in range(2):
                 xt = psum.tile([P, 4, P], F32, tag="xt", bufs=2, name="xt")
                 for i in range(2):
                     words = row_tiles[2 * pair + i].bitcast(F32)
                     for u in range(2):
                         nc.tensor.transpose(xt[:, 2 * i + u, :], words[:, P * u : P * (u + 1)], ident_f32[:])
-                nc.scalar.copy(
-                    out=grouped_words[:, 512 * pair : 512 * (pair + 1)].rearrange(
-                        "p (i c u) -> p i c u", i=2, u=2
-                    ),
-                    in_=xt[:].rearrange("p (i u) c -> p i c u", u=2),
-                )
-            return grouped
+                banks.append(xt)
+            return banks
+
+        def new_grouped():
+            return work.tile([P, TILES_PER_GROUP * P * PACK], BF16, tag="grouped", align_bytes=64, name="grouped")
+
+        def copy_out(banks, grouped, pair):
+            grouped_words = grouped[:].bitcast(F32)
+            nc.scalar.copy(
+                out=grouped_words[:, 512 * pair : 512 * (pair + 1)].rearrange("p (i c u) -> p i c u", i=2, u=2),
+                in_=banks[pair][:].rearrange("p (i u) c -> p i c u", u=2),
+            )
 
         def quantise(grouped, codes, scales):
             nc.vector.quantize_mx(out=codes.bitcast(FP8X4), scales=scales, in_=grouped)
 
         w1_codes = const.tile([P, PACK * P], U32, align_bytes=64)
         w1_scales = const.tile([P, PACK * P], U8, align_bytes=64)
-        w1_grouped = rows_to_grouped([w1_nodes[:, t, :] for t in range(PACK)])
+        w1_banks = transpose_rows([w1_nodes[:, t, :] for t in range(PACK)])
+        w1_grouped = new_grouped()
+        copy_out(w1_banks, w1_grouped, 0)
+        copy_out(w1_banks, w1_grouped, 1)
         quantise(w1_grouped[:], w1_codes[:], w1_scales[:])
 
         edge_terms = {}
 
-        def prepare_edge_term(q):
+        spreads = {}
+
+        def spread_edge(q):
             spread = psum.tile([P, TILES_PER_CHUNK, P], BF16, tag="spread", name="spread")
             for i in range(TILES_PER_CHUNK):
                 m = TILES_PER_CHUNK * q + i
                 nc.tensor.transpose(spread[:, i, :], edge_cols[:, m : m + 1].to_broadcast([P, P]), ident_bf[:])
+            spreads[q] = spread
+
+        def prepare_edge_term(q):
             edge_all = work.tile([P, TILES_PER_CHUNK, P], BF16, tag="edge_all", name="edge_all")
-            nc.scalar.copy(out=edge_all[:], in_=spread[:])
+            nc.scalar.copy(out=edge_all[:], in_=spreads[q][:])
             edge_term = work.tile([P, PACK, TILES_PER_CHUNK, P], F32, tag="edge_term", bufs=3, name="edge_term")
             for t in range(PACK):
                 nc.gpsimd.tensor_scalar(
@@ -167,19 +179,37 @@ def tile_edgenetwork_kernel(
         h_scales = {}
         sums2 = {}
 
+        x_banks = {}
+
+        def in_range(g):
+            return 0 <= g < N_GROUPS
+
         def transpose_x(g):
+            if not in_range(g):
+                return
             q, half = divmod(g, GROUPS_PER_CHUNK)
+            if half == 0 and q + CHUNKS_AHEAD < N_CHUNKS:
+                load_chunk(q + CHUNKS_AHEAD)
             x_sb = x_chunks[q]
-            x_grouped[g] = rows_to_grouped(
-                [x_sb[:, TILES_PER_GROUP * half + j, :] for j in range(TILES_PER_GROUP)]
-            )
+            x_banks[g] = transpose_rows([x_sb[:, TILES_PER_GROUP * half + j, :] for j in range(TILES_PER_GROUP)])
+
+        def copy_out_x(g, pair):
+            if not in_range(g):
+                return
+            if pair == 0:
+                x_grouped[g] = new_grouped()
+            copy_out(x_banks[g], x_grouped[g], pair)
 
         def quantise_x(g):
+            if not in_range(g):
+                return
             x_codes[g] = work.tile([P, TILES_PER_GROUP * P], U32, tag="x_codes", align_bytes=64, name="x_codes")
             x_scales[g] = work.tile([P, TILES_PER_GROUP * P], U8, tag="x_scales", align_bytes=64, name="x_scales")
             quantise(x_grouped[g][:], x_codes[g][:], x_scales[g][:])
 
         def layer1(g, j):
+            if not in_range(g):
+                return
             sums = psum.tile([P, PACK, P], F32, tag="sums1", bufs=4, name="sums")
             cols = slice(P * j, P * (j + 1))
             for t in range(PACK):
@@ -196,6 +226,8 @@ def tile_edgenetwork_kernel(
             sums1[(g, j)] = sums
 
         def hidden(g, j):
+            if not in_range(g):
+                return
             q, half = divmod(g, GROUPS_PER_CHUNK)
             if j == 0:
                 h_grouped[g] = work.tile([P, TILES_PER_GROUP, P * PACK], BF16, tag="h", bufs=3, align_bytes=64, name="h")
@@ -211,11 +243,15 @@ def tile_edgenetwork_kernel(
             )
 
         def quantise_h(g):
+            if not in_range(g):
+                return
             h_codes[g] = work.tile([P, TILES_PER_GROUP * P], U32, tag="h_codes", align_bytes=64, name="h_codes")
             h_scales[g] = work.tile([P, TILES_PER_GROUP * P], U8, tag="h_scales", align_bytes=64, name="h_scales")
             quantise(h_grouped[g][:].rearrange("p j w -> p (j w)"), h_codes[g][:], h_scales[g][:])
 
         def layer2(g):
+            if not in_range(g):
+                return
             sums = psum.tile([P, TILES_PER_GROUP, OUT], F32, tag="sums2", name="sums")
             for j in range(TILES_PER_GROUP):
                 cols = slice(P * j, P * (j + 1))
@@ -230,8 +266,11 @@ def tile_edgenetwork_kernel(
                 )
             sums2[g] = sums
 
-        def finish(g):
-            q, half = divmod(g, GROUPS_PER_CHUNK)
+        biased_sums = {}
+
+        def add_b2(g):
+            if not in_range(g):
+                return
             biased = work.tile([P, TILES_PER_GROUP, OUT], F32, tag="biased", name="biased")
             nc.vector.tensor_tensor(
                 out=biased[:],
@@ -239,29 +278,39 @@ def tile_edgenetwork_kernel(
                 in1=b2_f32[:].unsqueeze(1).to_broadcast([P, TILES_PER_GROUP, OUT]),
                 op=ALU.add,
             )
+            biased_sums[g] = biased
+
+        def tanh_and_store(g):
+            if not in_range(g):
+                return
+            q, half = divmod(g, GROUPS_PER_CHUNK)
             result = work.tile([P, TILES_PER_GROUP, OUT], F32, tag="result", bufs=3, name="result")
-            nc.scalar.activation(out=result[:], in_=biased[:], func=ACT.Tanh)
+            nc.scalar.activation(out=result[:], in_=biased_sums[g][:], func=ACT.Tanh)
             first = TILES_PER_GROUP * half
             nc.sync.dma_start(out=out_by_chunk[q][:, first : first + TILES_PER_GROUP, :], in_=result[:])
 
+        spread_edge(0)
         prepare_edge_term(0)
         for g in range(-2, N_GROUPS + 2):
-            if 0 <= g + 2 < N_GROUPS:
-                if (g + 2) % GROUPS_PER_CHUNK == 0 and (g + 2) // GROUPS_PER_CHUNK + CHUNKS_AHEAD < N_CHUNKS:
-                    load_chunk((g + 2) // GROUPS_PER_CHUNK + CHUNKS_AHEAD)
-                transpose_x(g + 2)
             ahead = g + EDGE_TERM_AHEAD
-            if ahead % GROUPS_PER_CHUNK == 0 and 0 < ahead < N_GROUPS:
+            new_edge_term = ahead % GROUPS_PER_CHUNK == 0 and 0 < ahead < N_GROUPS
+            transpose_x(g + 2)
+            if new_edge_term:
+                spread_edge(ahead // GROUPS_PER_CHUNK)
+            hidden(g, 0)
+            copy_out_x(g + 2, 0)
+            quantise_x(g + 1)
+            layer1(g + 1, 0)
+            hidden(g, 1)
+            copy_out_x(g + 2, 1)
+            if new_edge_term:
                 prepare_edge_term(ahead // GROUPS_PER_CHUNK)
-            if 0 <= g + 1 < N_GROUPS:
-                quantise_x(g + 1)
-            if 0 <= g - 2 < N_GROUPS:
-                finish(g - 2)
-            if 0 <= g - 1 < N_GROUPS:
-                quantise_h(g - 1)
-                layer2(g - 1)
-            for j in range(TILES_PER_GROUP):
-                if 0 <= g < N_GROUPS:
-                    hidden(g, j)
-                if 0 <= g + 1 < N_GROUPS:
-                    layer1(g + 1, j)
+            layer1(g + 1, 1)
+            add_b2(g - 2)
+            hidden(g, 2)
+            tanh_and_store(g - 2)
+            layer1(g + 1, 2)
+            quantise_h(g - 1)
+            layer2(g - 1)
+            hidden(g, 3)
+            layer1(g + 1, 3)

@@ -24,7 +24,7 @@ GROUPS_PER_CHUNK = TILES_PER_CHUNK // TILES_PER_GROUP
 N_CHUNKS = E // (P * TILES_PER_CHUNK)
 N_GROUPS = N_CHUNKS * GROUPS_PER_CHUNK
 CHUNKS_AHEAD = 3
-EDGE_TERM_AHEAD = 4
+EDGE_TERM_AHEAD = 5
 
 FLOPS = 2 * E * ((NODE + 1) * MID + MID * OUT)
 
@@ -144,18 +144,34 @@ def tile_edgenetwork_kernel(
         copy_out(w1_banks, w1_grouped, 1)
         quantise(w1_grouped[:], w1_codes[:], w1_scales[:])
 
+        def in_range(g):
+            return 0 <= g < N_GROUPS
+
         edge_terms = {}
 
         spreads = {}
 
-        def spread_edge(q):
-            spread = psum.tile([P, TILES_PER_CHUNK, P], BF16, tag="spread", name="spread")
-            for i in range(TILES_PER_CHUNK):
+        def spread_edge(g):
+            if not in_range(g):
+                return
+            q, half = divmod(g, GROUPS_PER_CHUNK)
+            if half == 0:
+                spreads[q] = psum.tile([P, TILES_PER_CHUNK, P], BF16, tag="spread", name="spread")
+            for j in range(TILES_PER_GROUP):
+                i = TILES_PER_GROUP * half + j
                 m = TILES_PER_CHUNK * q + i
-                nc.tensor.transpose(spread[:, i, :], edge_cols[:, m : m + 1].to_broadcast([P, P]), ident_bf[:])
-            spreads[q] = spread
+                nc.tensor.matmul(
+                    out=spreads[q][:, i, :],
+                    lhsT=edge_cols[:, m : m + 1].to_broadcast([P, P]),
+                    rhs=ident_bf[:],
+                    start=True,
+                    stop=True,
+                )
 
-        def prepare_edge_term(q):
+        def prepare_edge_term(g):
+            if not in_range(g) or g % GROUPS_PER_CHUNK != GROUPS_PER_CHUNK - 1:
+                return
+            q = g // GROUPS_PER_CHUNK
             edge_all = work.tile([P, TILES_PER_CHUNK, P], BF16, tag="edge_all", name="edge_all")
             nc.scalar.copy(out=edge_all[:], in_=spreads[q][:])
             edge_term = work.tile([P, PACK, TILES_PER_CHUNK, P], F32, tag="edge_term", bufs=3, name="edge_term")
@@ -180,9 +196,6 @@ def tile_edgenetwork_kernel(
         sums2 = {}
 
         x_banks = {}
-
-        def in_range(g):
-            return 0 <= g < N_GROUPS
 
         def transpose_x(g):
             if not in_range(g):
@@ -289,22 +302,19 @@ def tile_edgenetwork_kernel(
             first = TILES_PER_GROUP * half
             nc.sync.dma_start(out=out_by_chunk[q][:, first : first + TILES_PER_GROUP, :], in_=result[:])
 
-        spread_edge(0)
-        prepare_edge_term(0)
+        for g in range(-2 - EDGE_TERM_AHEAD, -2):
+            spread_edge(g + EDGE_TERM_AHEAD)
+            prepare_edge_term(g + EDGE_TERM_AHEAD)
         for g in range(-2, N_GROUPS + 2):
-            ahead = g + EDGE_TERM_AHEAD
-            new_edge_term = ahead % GROUPS_PER_CHUNK == 0 and 0 < ahead < N_GROUPS
             transpose_x(g + 2)
-            if new_edge_term:
-                spread_edge(ahead // GROUPS_PER_CHUNK)
+            spread_edge(g + EDGE_TERM_AHEAD)
             hidden(g, 0)
             copy_out_x(g + 2, 0)
             quantise_x(g + 1)
             layer1(g + 1, 0)
             hidden(g, 1)
             copy_out_x(g + 2, 1)
-            if new_edge_term:
-                prepare_edge_term(ahead // GROUPS_PER_CHUNK)
+            prepare_edge_term(g + EDGE_TERM_AHEAD)
             layer1(g + 1, 1)
             add_b2(g - 2)
             hidden(g, 2)

@@ -16,15 +16,16 @@ P = 128
 PACK = 4
 E, F, H, MID, OUT = 16384, 64, 192, 512, 128
 NODE = 2 * (F + H)
-NODE_WORDS = NODE // 2
 
 TILES_PER_GROUP = 4
 TILES_PER_CHUNK = 8
 GROUPS_PER_CHUNK = TILES_PER_CHUNK // TILES_PER_GROUP
 N_CHUNKS = E // (P * TILES_PER_CHUNK)
 N_GROUPS = N_CHUNKS * GROUPS_PER_CHUNK
+N_TILES = N_GROUPS * TILES_PER_GROUP
 CHUNKS_AHEAD = 3
-EDGE_TERM_AHEAD = 5
+SUMS1_BANKS = 3
+EDGE_TERM_AHEAD = 3
 
 FLOPS = 2 * E * ((NODE + 1) * MID + MID * OUT)
 
@@ -73,15 +74,15 @@ def tile_edgenetwork_kernel(
         w1_rows = const.tile([P, PACK, NODE + 1], BF16)
         nc.sync.dma_start(out=w1_rows[:], in_=W1.rearrange("(j t) k -> j t k", t=PACK))
         load_chunk(0)
-        edge_cols = const.tile([P, N_CHUNKS * TILES_PER_CHUNK], BF16)
+        edge_cols = const.tile([P, N_TILES], BF16)
         nc.scalar.dma_start(
             out=edge_cols[:].rearrange("c (q i) -> c q i", i=TILES_PER_CHUNK),
             in_=edge_feat.rearrange("(q c i) -> c q i", c=P, i=TILES_PER_CHUNK),
         )
         b1_bf = const.tile([P, PACK], BF16)
         nc.scalar.dma_start(out=b1_bf[:], in_=b1.rearrange("(p t) -> p t", t=PACK))
-        b2_bf = const.tile([P, OUT], BF16)
-        nc.scalar.dma_start(out=b2_bf[:], in_=b2.partition_broadcast(P))
+        b2_bf = const.tile([P, 1], BF16)
+        nc.scalar.dma_start(out=b2_bf[:], in_=b2.rearrange("(p o) -> p o", o=1))
         load_chunk(1)
 
         w2_codes = const.tile([P, OUT * PACK], U8, align_bytes=64)
@@ -109,8 +110,11 @@ def tile_edgenetwork_kernel(
         nc.vector.tensor_copy(out=w1_edge[:], in_=w1_rows[:, :, NODE])
         b1_f32 = const.tile([P, PACK], F32)
         nc.vector.tensor_copy(out=b1_f32[:], in_=b1_bf[:])
-        b2_f32 = const.tile([P, OUT], F32)
+        b2_f32 = const.tile([P, 1], F32)
         nc.vector.tensor_copy(out=b2_f32[:], in_=b2_bf[:])
+
+        def group_in_range(g):
+            return 0 <= g < N_GROUPS
 
         def transpose_rows(row_tiles):
             banks = []
@@ -144,61 +148,54 @@ def tile_edgenetwork_kernel(
         copy_out(w1_banks, w1_grouped, 1)
         quantise(w1_grouped[:], w1_codes[:], w1_scales[:])
 
-        def in_range(g):
-            return 0 <= g < N_GROUPS
-
+        spreads = {}
         edge_terms = {}
 
-        spreads = {}
-
         def spread_edge(g):
-            if not in_range(g):
+            if not group_in_range(g) or g % GROUPS_PER_CHUNK != 0:
                 return
-            q, half = divmod(g, GROUPS_PER_CHUNK)
-            if half == 0:
-                spreads[q] = psum.tile([P, TILES_PER_CHUNK, P], BF16, tag="spread", name="spread")
-            for j in range(TILES_PER_GROUP):
-                i = TILES_PER_GROUP * half + j
+            q = g // GROUPS_PER_CHUNK
+            spread = psum.tile([P, TILES_PER_CHUNK, P], BF16, tag="spread", name="spread")
+            for i in range(TILES_PER_CHUNK):
                 m = TILES_PER_CHUNK * q + i
                 nc.tensor.matmul(
-                    out=spreads[q][:, i, :],
+                    out=spread[:, i, :],
                     lhsT=edge_cols[:, m : m + 1].to_broadcast([P, P]),
                     rhs=ident_bf[:],
                     start=True,
                     stop=True,
                 )
+            spreads[q] = spread
+            edge_terms[q] = work.tile([P, PACK, TILES_PER_CHUNK, P], F32, tag="edge_term", bufs=3, name="edge_term")
 
-        def prepare_edge_term(g):
-            if not in_range(g) or g % GROUPS_PER_CHUNK != GROUPS_PER_CHUNK - 1:
+        def edge_term_block(g, part):
+            if not group_in_range(g):
                 return
-            q = g // GROUPS_PER_CHUNK
-            edge_all = work.tile([P, TILES_PER_CHUNK, P], BF16, tag="edge_all", name="edge_all")
-            nc.scalar.copy(out=edge_all[:], in_=spreads[q][:])
-            edge_term = work.tile([P, PACK, TILES_PER_CHUNK, P], F32, tag="edge_term", bufs=3, name="edge_term")
-            for t in range(PACK):
-                nc.gpsimd.tensor_scalar(
-                    out=edge_term[:, t, :, :],
-                    in0=edge_all[:],
-                    scalar1=w1_edge[:, t : t + 1],
-                    scalar2=b1_f32[:, t : t + 1],
-                    op0=ALU.mult,
-                    op1=ALU.add,
-                )
-            edge_terms[q] = edge_term
+            q, half = divmod(g, GROUPS_PER_CHUNK)
+            t = 2 * half + part
+            nc.scalar.activation(
+                out=edge_terms[q][:, t, :, :],
+                in_=spreads[q][:],
+                func=ACT.Identity,
+                scale=w1_edge[:, t : t + 1],
+                bias=b1_f32[:, t : t + 1],
+            )
 
+        x_banks = {}
         x_grouped = {}
         x_codes = {}
         x_scales = {}
         sums1 = {}
+        pre_grouped = {}
         h_grouped = {}
         h_codes = {}
         h_scales = {}
         sums2 = {}
-
-        x_banks = {}
+        out_rows = {}
+        out_banks = {}
 
         def transpose_x(g):
-            if not in_range(g):
+            if not group_in_range(g):
                 return
             q, half = divmod(g, GROUPS_PER_CHUNK)
             if half == 0 and q + CHUNKS_AHEAD < N_CHUNKS:
@@ -207,23 +204,24 @@ def tile_edgenetwork_kernel(
             x_banks[g] = transpose_rows([x_sb[:, TILES_PER_GROUP * half + j, :] for j in range(TILES_PER_GROUP)])
 
         def copy_out_x(g, pair):
-            if not in_range(g):
+            if not group_in_range(g):
                 return
             if pair == 0:
                 x_grouped[g] = new_grouped()
             copy_out(x_banks[g], x_grouped[g], pair)
 
         def quantise_x(g):
-            if not in_range(g):
+            if not group_in_range(g):
                 return
             x_codes[g] = work.tile([P, TILES_PER_GROUP * P], U32, tag="x_codes", align_bytes=64, name="x_codes")
             x_scales[g] = work.tile([P, TILES_PER_GROUP * P], U8, tag="x_scales", align_bytes=64, name="x_scales")
             quantise(x_grouped[g][:], x_codes[g][:], x_scales[g][:])
 
-        def layer1(g, j):
-            if not in_range(g):
+        def layer1(n):
+            if not 0 <= n < N_TILES:
                 return
-            sums = psum.tile([P, PACK, P], F32, tag="sums1", bufs=4, name="sums")
+            g, j = divmod(n, TILES_PER_GROUP)
+            sums = psum.tile([P, PACK, P], F32, tag="sums1", bufs=SUMS1_BANKS, name="sums1_tile")
             cols = slice(P * j, P * (j + 1))
             for t in range(PACK):
                 block = slice(P * t, P * (t + 1))
@@ -236,91 +234,95 @@ def tile_edgenetwork_kernel(
                     start=True,
                     stop=True,
                 )
-            sums1[(g, j)] = sums
+            sums1[n] = sums
 
-        def hidden(g, j):
-            if not in_range(g):
+        def add_edge_term(n):
+            if not 0 <= n < N_TILES:
                 return
-            q, half = divmod(g, GROUPS_PER_CHUNK)
+            g, j = divmod(n, TILES_PER_GROUP)
+            q, i = divmod(n, TILES_PER_CHUNK)
             if j == 0:
-                h_grouped[g] = work.tile([P, TILES_PER_GROUP, P * PACK], BF16, tag="h", bufs=3, align_bytes=64, name="h")
-            pre = work.tile([P, P, PACK], BF16, tag="pre", bufs=3, name="pre")
+                pre_grouped[g] = work.tile([P, TILES_PER_GROUP, P, PACK], BF16, tag="pre", name="pre")
             nc.vector.tensor_tensor(
-                out=pre[:],
-                in0=sums1[(g, j)][:].rearrange("p t c -> p c t"),
-                in1=edge_terms[q][:, :, TILES_PER_GROUP * half + j, :].rearrange("p t c -> p c t"),
+                out=pre_grouped[g][:, j, :, :],
+                in0=sums1[n][:].rearrange("p t c -> p c t"),
+                in1=edge_terms[q][:, :, i, :].rearrange("p t c -> p c t"),
                 op=ALU.add,
             )
-            nc.scalar.activation(
-                out=h_grouped[g][:, j, :], in_=pre[:].rearrange("p c t -> p (c t)"), func=ACT.Relu
+
+        def relu(g):
+            if not group_in_range(g):
+                return
+            h_grouped[g] = work.tile([P, TILES_PER_GROUP * P * PACK], BF16, tag="h", align_bytes=64, name="h")
+            nc.vector.tensor_scalar_max(
+                out=h_grouped[g][:], in0=pre_grouped[g][:].rearrange("p j c t -> p (j c t)"), scalar1=0.0
             )
 
         def quantise_h(g):
-            if not in_range(g):
+            if not group_in_range(g):
                 return
             h_codes[g] = work.tile([P, TILES_PER_GROUP * P], U32, tag="h_codes", align_bytes=64, name="h_codes")
             h_scales[g] = work.tile([P, TILES_PER_GROUP * P], U8, tag="h_scales", align_bytes=64, name="h_scales")
-            quantise(h_grouped[g][:].rearrange("p j w -> p (j w)"), h_codes[g][:], h_scales[g][:])
+            quantise(h_grouped[g][:], h_codes[g][:], h_scales[g][:])
 
         def layer2(g):
-            if not in_range(g):
+            if not group_in_range(g):
                 return
-            sums = psum.tile([P, TILES_PER_GROUP, OUT], F32, tag="sums2", name="sums")
-            for j in range(TILES_PER_GROUP):
-                cols = slice(P * j, P * (j + 1))
-                nc.tensor.matmul_mx(
-                    out=sums[:, j, :],
-                    lhsT=h_codes[g][:, cols].bitcast(FP8X4),
-                    lhsT_scale=h_scales[g][:, cols],
-                    rhs=w2_codes[:].bitcast(FP8X4),
-                    rhs_scale=w2_scales[:],
-                    start=True,
-                    stop=True,
-                )
+            sums = psum.tile([P, TILES_PER_GROUP * P], F32, tag="sums2", name="sums2_tile")
+            nc.tensor.matmul_mx(
+                out=sums[:],
+                lhsT=w2_codes[:].bitcast(FP8X4),
+                lhsT_scale=w2_scales[:],
+                rhs=h_codes[g][:].bitcast(FP8X4),
+                rhs_scale=h_scales[g][:],
+                start=True,
+                stop=True,
+            )
             sums2[g] = sums
 
-        biased_sums = {}
-
-        def add_b2(g):
-            if not in_range(g):
+        def tanh(g):
+            if not group_in_range(g):
                 return
-            biased = work.tile([P, TILES_PER_GROUP, OUT], F32, tag="biased", name="biased")
-            nc.vector.tensor_tensor(
-                out=biased[:],
-                in0=sums2[g][:],
-                in1=b2_f32[:].unsqueeze(1).to_broadcast([P, TILES_PER_GROUP, OUT]),
-                op=ALU.add,
-            )
-            biased_sums[g] = biased
+            out_rows[g] = work.tile([P, TILES_PER_GROUP * P], F32, tag="out_rows", name="out_rows")
+            nc.scalar.activation(out=out_rows[g][:], in_=sums2[g][:], func=ACT.Tanh, bias=b2_f32[:, 0:1])
 
-        def tanh_and_store(g):
-            if not in_range(g):
+        def transpose_out(g):
+            if not group_in_range(g):
+                return
+            bank = psum.tile([P, TILES_PER_GROUP, OUT], F32, tag="out_bank", name="out_bank")
+            for j in range(TILES_PER_GROUP):
+                nc.tensor.transpose(bank[:, j, :], out_rows[g][:, P * j : P * (j + 1)], ident_f32[:])
+            out_banks[g] = bank
+
+        def store(g):
+            if not group_in_range(g):
                 return
             q, half = divmod(g, GROUPS_PER_CHUNK)
             result = work.tile([P, TILES_PER_GROUP, OUT], F32, tag="result", bufs=3, name="result")
-            nc.scalar.activation(out=result[:], in_=biased_sums[g][:], func=ACT.Tanh)
+            nc.scalar.copy(out=result[:], in_=out_banks[g][:])
             first = TILES_PER_GROUP * half
             nc.sync.dma_start(out=out_by_chunk[q][:, first : first + TILES_PER_GROUP, :], in_=result[:])
 
-        for g in range(-2 - EDGE_TERM_AHEAD, -2):
-            spread_edge(g + EDGE_TERM_AHEAD)
-            prepare_edge_term(g + EDGE_TERM_AHEAD)
-        for g in range(-2, N_GROUPS + 2):
+        for g in range(-EDGE_TERM_AHEAD - 1, N_GROUPS + 2):
+            first_tile = TILES_PER_GROUP * g
             transpose_x(g + 2)
-            spread_edge(g + EDGE_TERM_AHEAD)
-            hidden(g, 0)
+            transpose_out(g - 2)
+            edge_term_block(g + EDGE_TERM_AHEAD, 0)
+            add_edge_term(first_tile)
+            layer1(first_tile + SUMS1_BANKS)
             copy_out_x(g + 2, 0)
             quantise_x(g + 1)
-            layer1(g + 1, 0)
-            hidden(g, 1)
-            copy_out_x(g + 2, 1)
-            prepare_edge_term(g + EDGE_TERM_AHEAD)
-            layer1(g + 1, 1)
-            add_b2(g - 2)
-            hidden(g, 2)
-            tanh_and_store(g - 2)
-            layer1(g + 1, 2)
+            add_edge_term(first_tile + 1)
+            layer1(first_tile + 1 + SUMS1_BANKS)
+            store(g - 2)
+            add_edge_term(first_tile + 2)
+            layer1(first_tile + 2 + SUMS1_BANKS)
+            edge_term_block(g + EDGE_TERM_AHEAD, 1)
             quantise_h(g - 1)
             layer2(g - 1)
-            hidden(g, 3)
-            layer1(g + 1, 3)
+            copy_out_x(g + 2, 1)
+            add_edge_term(first_tile + 3)
+            layer1(first_tile + 3 + SUMS1_BANKS)
+            spread_edge(g + EDGE_TERM_AHEAD + 1)
+            relu(g)
+            tanh(g - 1)

@@ -16,16 +16,17 @@ P = 128
 PACK = 4
 E, F, H, MID, OUT = 16384, 64, 192, 512, 128
 NODE = 2 * (F + H)
+NODE_WORDS = NODE // 2
 
 TILES_PER_GROUP = 4
 TILES_PER_CHUNK = 8
 GROUPS_PER_CHUNK = TILES_PER_CHUNK // TILES_PER_GROUP
 N_CHUNKS = E // (P * TILES_PER_CHUNK)
 N_GROUPS = N_CHUNKS * GROUPS_PER_CHUNK
-N_TILES = N_GROUPS * TILES_PER_GROUP
 CHUNKS_AHEAD = 3
-SUMS1_BANKS = 3
-EDGE_TERM_AHEAD = 3
+EDGE_TERM_AHEAD = 5
+
+RUN = 4
 
 FLOPS = 2 * E * ((NODE + 1) * MID + MID * OUT)
 
@@ -50,10 +51,12 @@ def tile_edgenetwork_kernel(
         return rows.rearrange("(q c i) f -> q c i f", c=P, i=TILES_PER_CHUNK)
 
     node_inputs = (
-        (by_chunk(dst_node_feat), 0, F),
-        (by_chunk(dst_node_hidden), F, H),
-        (by_chunk(src_node_feat), F + H, F),
-        (by_chunk(src_node_hidden), 2 * F + H, H),
+        (by_chunk(dst_node_feat), 0, 0, F),
+        (by_chunk(dst_node_hidden), 0, F, 2 * F),
+        (by_chunk(dst_node_hidden), 2 * F, 3 * F, F),
+        (by_chunk(src_node_feat), 0, F + H, F),
+        (by_chunk(src_node_hidden), 0, 2 * F + H, 2 * F),
+        (by_chunk(src_node_hidden), 2 * F, 4 * F + H, F),
     )
     out_by_chunk = by_chunk(out)
 
@@ -67,22 +70,24 @@ def tile_edgenetwork_kernel(
 
         def load_chunk(q):
             x_sb = work.tile([P, TILES_PER_CHUNK, NODE], BF16, tag="x", bufs=CHUNKS_AHEAD + 1, name="x_sb")
-            for rows, first, width in node_inputs:
-                nc.sync.dma_start(out=x_sb[:, :, first : first + width], in_=rows[q])
+            for rows, first_in, first_x, width in node_inputs:
+                nc.sync.dma_start(
+                    out=x_sb[:, :, first_x : first_x + width], in_=rows[q][:, :, first_in : first_in + width]
+                )
             x_chunks[q] = x_sb
 
         w1_rows = const.tile([P, PACK, NODE + 1], BF16)
         nc.sync.dma_start(out=w1_rows[:], in_=W1.rearrange("(j t) k -> j t k", t=PACK))
         load_chunk(0)
-        edge_cols = const.tile([P, N_TILES], BF16)
+        edge_cols = const.tile([P, N_CHUNKS * TILES_PER_CHUNK], BF16)
         nc.scalar.dma_start(
             out=edge_cols[:].rearrange("c (q i) -> c q i", i=TILES_PER_CHUNK),
             in_=edge_feat.rearrange("(q c i) -> c q i", c=P, i=TILES_PER_CHUNK),
         )
         b1_bf = const.tile([P, PACK], BF16)
         nc.scalar.dma_start(out=b1_bf[:], in_=b1.rearrange("(p t) -> p t", t=PACK))
-        b2_bf = const.tile([P, 1], BF16)
-        nc.scalar.dma_start(out=b2_bf[:], in_=b2.rearrange("(p o) -> p o", o=1))
+        b2_bf = const.tile([P, OUT], BF16)
+        nc.scalar.dma_start(out=b2_bf[:], in_=b2.partition_broadcast(P))
         load_chunk(1)
 
         w2_codes = const.tile([P, OUT * PACK], U8, align_bytes=64)
@@ -110,11 +115,8 @@ def tile_edgenetwork_kernel(
         nc.vector.tensor_copy(out=w1_edge[:], in_=w1_rows[:, :, NODE])
         b1_f32 = const.tile([P, PACK], F32)
         nc.vector.tensor_copy(out=b1_f32[:], in_=b1_bf[:])
-        b2_f32 = const.tile([P, 1], F32)
+        b2_f32 = const.tile([P, OUT], F32)
         nc.vector.tensor_copy(out=b2_f32[:], in_=b2_bf[:])
-
-        def group_in_range(g):
-            return 0 <= g < N_GROUPS
 
         def transpose_rows(row_tiles):
             banks = []
@@ -148,54 +150,61 @@ def tile_edgenetwork_kernel(
         copy_out(w1_banks, w1_grouped, 1)
         quantise(w1_grouped[:], w1_codes[:], w1_scales[:])
 
-        spreads = {}
+        def in_range(g):
+            return 0 <= g < N_GROUPS
+
         edge_terms = {}
 
+        spreads = {}
+
         def spread_edge(g):
-            if not group_in_range(g) or g % GROUPS_PER_CHUNK != 0:
+            if not in_range(g):
                 return
-            q = g // GROUPS_PER_CHUNK
-            spread = psum.tile([P, TILES_PER_CHUNK, P], BF16, tag="spread", name="spread")
-            for i in range(TILES_PER_CHUNK):
+            q, half = divmod(g, GROUPS_PER_CHUNK)
+            if half == 0:
+                spreads[q] = psum.tile([P, TILES_PER_CHUNK, P], BF16, tag="spread", name="spread")
+            for j in range(TILES_PER_GROUP):
+                i = TILES_PER_GROUP * half + j
                 m = TILES_PER_CHUNK * q + i
                 nc.tensor.matmul(
-                    out=spread[:, i, :],
+                    out=spreads[q][:, i, :],
                     lhsT=edge_cols[:, m : m + 1].to_broadcast([P, P]),
                     rhs=ident_bf[:],
                     start=True,
                     stop=True,
                 )
-            spreads[q] = spread
-            edge_terms[q] = work.tile([P, PACK, TILES_PER_CHUNK, P], F32, tag="edge_term", bufs=3, name="edge_term")
 
-        def edge_term_block(g, part):
-            if not group_in_range(g):
+        def prepare_edge_term(g):
+            if not in_range(g) or g % GROUPS_PER_CHUNK != GROUPS_PER_CHUNK - 1:
                 return
-            q, half = divmod(g, GROUPS_PER_CHUNK)
-            t = 2 * half + part
-            nc.scalar.activation(
-                out=edge_terms[q][:, t, :, :],
-                in_=spreads[q][:],
-                func=ACT.Identity,
-                scale=w1_edge[:, t : t + 1],
-                bias=b1_f32[:, t : t + 1],
-            )
+            q = g // GROUPS_PER_CHUNK
+            edge_all = work.tile([P, TILES_PER_CHUNK, P], BF16, tag="edge_all", name="edge_all")
+            nc.scalar.copy(out=edge_all[:], in_=spreads[q][:])
+            edge_term = work.tile([P, PACK, TILES_PER_CHUNK, P], F32, tag="edge_term", bufs=3, name="edge_term")
+            for t in range(PACK):
+                nc.gpsimd.tensor_scalar(
+                    out=edge_term[:, t, :, :],
+                    in0=edge_all[:],
+                    scalar1=w1_edge[:, t : t + 1],
+                    scalar2=b1_f32[:, t : t + 1],
+                    op0=ALU.mult,
+                    op1=ALU.add,
+                )
+            edge_terms[q] = edge_term
 
-        x_banks = {}
         x_grouped = {}
         x_codes = {}
         x_scales = {}
         sums1 = {}
-        pre_grouped = {}
         h_grouped = {}
         h_codes = {}
         h_scales = {}
         sums2 = {}
-        out_rows = {}
-        out_banks = {}
+
+        x_banks = {}
 
         def transpose_x(g):
-            if not group_in_range(g):
+            if not in_range(g):
                 return
             q, half = divmod(g, GROUPS_PER_CHUNK)
             if half == 0 and q + CHUNKS_AHEAD < N_CHUNKS:
@@ -204,24 +213,23 @@ def tile_edgenetwork_kernel(
             x_banks[g] = transpose_rows([x_sb[:, TILES_PER_GROUP * half + j, :] for j in range(TILES_PER_GROUP)])
 
         def copy_out_x(g, pair):
-            if not group_in_range(g):
+            if not in_range(g):
                 return
             if pair == 0:
                 x_grouped[g] = new_grouped()
             copy_out(x_banks[g], x_grouped[g], pair)
 
         def quantise_x(g):
-            if not group_in_range(g):
+            if not in_range(g):
                 return
             x_codes[g] = work.tile([P, TILES_PER_GROUP * P], U32, tag="x_codes", align_bytes=64, name="x_codes")
             x_scales[g] = work.tile([P, TILES_PER_GROUP * P], U8, tag="x_scales", align_bytes=64, name="x_scales")
             quantise(x_grouped[g][:], x_codes[g][:], x_scales[g][:])
 
-        def layer1(n):
-            if not 0 <= n < N_TILES:
+        def layer1(g, j):
+            if not in_range(g):
                 return
-            g, j = divmod(n, TILES_PER_GROUP)
-            sums = psum.tile([P, PACK, P], F32, tag="sums1", bufs=SUMS1_BANKS, name="sums1_tile")
+            sums = psum.tile([P, PACK, P], F32, tag="sums1", bufs=4, name="sums")
             cols = slice(P * j, P * (j + 1))
             for t in range(PACK):
                 block = slice(P * t, P * (t + 1))
@@ -234,95 +242,91 @@ def tile_edgenetwork_kernel(
                     start=True,
                     stop=True,
                 )
-            sums1[n] = sums
+            sums1[(g, j)] = sums
 
-        def add_edge_term(n):
-            if not 0 <= n < N_TILES:
+        def hidden(g, j):
+            if not in_range(g):
                 return
-            g, j = divmod(n, TILES_PER_GROUP)
-            q, i = divmod(n, TILES_PER_CHUNK)
+            q, half = divmod(g, GROUPS_PER_CHUNK)
             if j == 0:
-                pre_grouped[g] = work.tile([P, TILES_PER_GROUP, P, PACK], BF16, tag="pre", name="pre")
+                h_grouped[g] = work.tile([P, TILES_PER_GROUP, P * PACK], BF16, tag="h", bufs=3, align_bytes=64, name="h")
+            pre = work.tile([P, P, PACK], BF16, tag="pre", bufs=3, name="pre")
             nc.vector.tensor_tensor(
-                out=pre_grouped[g][:, j, :, :],
-                in0=sums1[n][:].rearrange("p t c -> p c t"),
-                in1=edge_terms[q][:, :, i, :].rearrange("p t c -> p c t"),
+                out=pre[:].rearrange("p (b i) t -> p b t i", i=RUN),
+                in0=sums1[(g, j)][:].rearrange("p t (b i) -> p b t i", i=RUN),
+                in1=edge_terms[q][:, :, TILES_PER_GROUP * half + j, :].rearrange("p t (b i) -> p b t i", i=RUN),
                 op=ALU.add,
             )
-
-        def relu(g):
-            if not group_in_range(g):
-                return
-            h_grouped[g] = work.tile([P, TILES_PER_GROUP * P * PACK], BF16, tag="h", align_bytes=64, name="h")
-            nc.vector.tensor_scalar_max(
-                out=h_grouped[g][:], in0=pre_grouped[g][:].rearrange("p j c t -> p (j c t)"), scalar1=0.0
+            nc.scalar.activation(
+                out=h_grouped[g][:, j, :], in_=pre[:].rearrange("p c t -> p (c t)"), func=ACT.Relu
             )
 
         def quantise_h(g):
-            if not group_in_range(g):
+            if not in_range(g):
                 return
             h_codes[g] = work.tile([P, TILES_PER_GROUP * P], U32, tag="h_codes", align_bytes=64, name="h_codes")
             h_scales[g] = work.tile([P, TILES_PER_GROUP * P], U8, tag="h_scales", align_bytes=64, name="h_scales")
-            quantise(h_grouped[g][:], h_codes[g][:], h_scales[g][:])
+            quantise(h_grouped[g][:].rearrange("p j w -> p (j w)"), h_codes[g][:], h_scales[g][:])
 
         def layer2(g):
-            if not group_in_range(g):
+            if not in_range(g):
                 return
-            sums = psum.tile([P, TILES_PER_GROUP * P], F32, tag="sums2", name="sums2_tile")
-            nc.tensor.matmul_mx(
-                out=sums[:],
-                lhsT=w2_codes[:].bitcast(FP8X4),
-                lhsT_scale=w2_scales[:],
-                rhs=h_codes[g][:].bitcast(FP8X4),
-                rhs_scale=h_scales[g][:],
-                start=True,
-                stop=True,
-            )
+            sums = psum.tile([P, TILES_PER_GROUP, OUT], F32, tag="sums2", name="sums")
+            for j in range(TILES_PER_GROUP):
+                cols = slice(P * j, P * (j + 1))
+                nc.tensor.matmul_mx(
+                    out=sums[:, j, :],
+                    lhsT=h_codes[g][:, cols].bitcast(FP8X4),
+                    lhsT_scale=h_scales[g][:, cols],
+                    rhs=w2_codes[:].bitcast(FP8X4),
+                    rhs_scale=w2_scales[:],
+                    start=True,
+                    stop=True,
+                )
             sums2[g] = sums
 
-        def tanh(g):
-            if not group_in_range(g):
-                return
-            out_rows[g] = work.tile([P, TILES_PER_GROUP * P], F32, tag="out_rows", name="out_rows")
-            nc.scalar.activation(out=out_rows[g][:], in_=sums2[g][:], func=ACT.Tanh, bias=b2_f32[:, 0:1])
+        biased_sums = {}
 
-        def transpose_out(g):
-            if not group_in_range(g):
+        def add_b2(g):
+            if not in_range(g):
                 return
-            bank = psum.tile([P, TILES_PER_GROUP, OUT], F32, tag="out_bank", name="out_bank")
-            for j in range(TILES_PER_GROUP):
-                nc.tensor.transpose(bank[:, j, :], out_rows[g][:, P * j : P * (j + 1)], ident_f32[:])
-            out_banks[g] = bank
+            biased = work.tile([P, TILES_PER_GROUP, OUT], F32, tag="biased", name="biased")
+            nc.vector.tensor_tensor(
+                out=biased[:],
+                in0=sums2[g][:],
+                in1=b2_f32[:].unsqueeze(1).to_broadcast([P, TILES_PER_GROUP, OUT]),
+                op=ALU.add,
+            )
+            biased_sums[g] = biased
 
-        def store(g):
-            if not group_in_range(g):
+        def tanh_and_store(g):
+            if not in_range(g):
                 return
             q, half = divmod(g, GROUPS_PER_CHUNK)
             result = work.tile([P, TILES_PER_GROUP, OUT], F32, tag="result", bufs=3, name="result")
-            nc.scalar.copy(out=result[:], in_=out_banks[g][:])
+            nc.scalar.activation(out=result[:], in_=biased_sums[g][:], func=ACT.Tanh)
             first = TILES_PER_GROUP * half
             nc.sync.dma_start(out=out_by_chunk[q][:, first : first + TILES_PER_GROUP, :], in_=result[:])
 
-        for g in range(-EDGE_TERM_AHEAD - 1, N_GROUPS + 2):
-            first_tile = TILES_PER_GROUP * g
+        for g in range(-2 - EDGE_TERM_AHEAD, -2):
+            spread_edge(g + EDGE_TERM_AHEAD)
+            prepare_edge_term(g + EDGE_TERM_AHEAD)
+        for g in range(-2, N_GROUPS + 2):
             transpose_x(g + 2)
-            transpose_out(g - 2)
-            edge_term_block(g + EDGE_TERM_AHEAD, 0)
-            add_edge_term(first_tile)
-            layer1(first_tile + SUMS1_BANKS)
+            spread_edge(g + EDGE_TERM_AHEAD)
+            hidden(g, 0)
             copy_out_x(g + 2, 0)
             quantise_x(g + 1)
-            add_edge_term(first_tile + 1)
-            layer1(first_tile + 1 + SUMS1_BANKS)
-            store(g - 2)
-            add_edge_term(first_tile + 2)
-            layer1(first_tile + 2 + SUMS1_BANKS)
-            edge_term_block(g + EDGE_TERM_AHEAD, 1)
+            layer1(g + 1, 0)
+            hidden(g, 1)
+            copy_out_x(g + 2, 1)
+            prepare_edge_term(g + EDGE_TERM_AHEAD)
+            layer1(g + 1, 1)
+            add_b2(g - 2)
+            hidden(g, 2)
+            tanh_and_store(g - 2)
+            layer1(g + 1, 2)
             quantise_h(g - 1)
             layer2(g - 1)
-            copy_out_x(g + 2, 1)
-            add_edge_term(first_tile + 3)
-            layer1(first_tile + 3 + SUMS1_BANKS)
-            spread_edge(g + EDGE_TERM_AHEAD + 1)
-            relu(g)
-            tanh(g - 1)
+            hidden(g, 3)
+            layer1(g + 1, 3)

@@ -250,15 +250,17 @@ def tile_edgenetwork_kernel(
             q, half = divmod(g, GROUPS_PER_CHUNK)
             if j == 0:
                 h_grouped[g] = work.tile([P, TILES_PER_GROUP, P * PACK], BF16, tag="h", bufs=3, align_bytes=64, name="h")
-            pre = work.tile([P, P, PACK], BF16, tag="pre", bufs=3, name="pre")
+            pre = work.tile([P, PACK, P], BF16, tag="pre", bufs=3, name="pre")
             nc.vector.tensor_tensor(
-                out=pre[:].rearrange("p (b i) t -> p b t i", i=RUN),
-                in0=sums1[(g, j)][:].rearrange("p t (b i) -> p b t i", i=RUN),
-                in1=edge_terms[q][:, :, TILES_PER_GROUP * half + j, :].rearrange("p t (b i) -> p b t i", i=RUN),
+                out=pre[:],
+                in0=sums1[(g, j)][:],
+                in1=edge_terms[q][:, :, TILES_PER_GROUP * half + j, :],
                 op=ALU.add,
             )
             nc.scalar.activation(
-                out=h_grouped[g][:, j, :], in_=pre[:].rearrange("p c t -> p (c t)"), func=ACT.Relu
+                out=h_grouped[g][:, j, :].rearrange("p (b i t) -> p b t i", i=RUN, t=PACK),
+                in_=pre[:].rearrange("p t (b i) -> p b t i", i=RUN),
+                func=ACT.Relu,
             )
 
         def quantise_h(g):

@@ -50,14 +50,13 @@ def tile_edgenetwork_kernel(
     def by_chunk(rows):
         return rows.rearrange("(q c i) f -> q c i f", c=P, i=TILES_PER_CHUNK)
 
-    node_inputs = (
-        (by_chunk(dst_node_feat), 0, 0, F),
+    hidden_inputs = (
         (by_chunk(dst_node_hidden), 0, F, 2 * F),
         (by_chunk(dst_node_hidden), 2 * F, 3 * F, F),
-        (by_chunk(src_node_feat), 0, F + H, F),
         (by_chunk(src_node_hidden), 0, 2 * F + H, 2 * F),
         (by_chunk(src_node_hidden), 2 * F, 4 * F + H, F),
     )
+    feat_inputs = (by_chunk(dst_node_feat), by_chunk(src_node_feat))
     out_by_chunk = by_chunk(out)
 
     with ExitStack() as stack:
@@ -68,13 +67,28 @@ def tile_edgenetwork_kernel(
 
         x_chunks = {}
 
+        feat_chunks = {}
+
         def load_chunk(q):
             x_sb = work.tile([P, TILES_PER_CHUNK, NODE], BF16, tag="x", bufs=CHUNKS_AHEAD + 1, name="x_sb")
-            for rows, first_in, first_x, width in node_inputs:
+            for rows, first_in, first_x, width in hidden_inputs:
                 nc.sync.dma_start(
                     out=x_sb[:, :, first_x : first_x + width], in_=rows[q][:, :, first_in : first_in + width]
                 )
+            feats = work.tile([P, 2, TILES_PER_CHUNK, F], BF16, tag="feats", bufs=CHUNKS_AHEAD + 1, name="feats")
+            for side, rows in enumerate(feat_inputs):
+                nc.sync.dma_start(out=feats[:, side, :, :], in_=rows[q])
             x_chunks[q] = x_sb
+            feat_chunks[q] = feats
+
+        def place_feats(g):
+            if not 0 <= g < N_GROUPS or g % GROUPS_PER_CHUNK != 0:
+                return
+            q = g // GROUPS_PER_CHUNK
+            nc.vector.tensor_copy(
+                out=x_chunks[q][:].rearrange("p i (side k) -> p side i k", side=2)[:, :, :, 0:F],
+                in_=feat_chunks[q][:],
+            )
 
         w1_rows = const.tile([P, PACK, NODE + 1], BF16)
         nc.sync.dma_start(out=w1_rows[:], in_=W1.rearrange("(j t) k -> j t k", t=PACK))
@@ -117,6 +131,7 @@ def tile_edgenetwork_kernel(
         nc.vector.tensor_copy(out=b1_f32[:], in_=b1_bf[:])
         b2_f32 = const.tile([P, OUT], F32)
         nc.vector.tensor_copy(out=b2_f32[:], in_=b2_bf[:])
+        place_feats(0)
 
         def transpose_rows(row_tiles):
             banks = []
@@ -332,3 +347,4 @@ def tile_edgenetwork_kernel(
             layer2(g - 1)
             hidden(g, 3)
             layer1(g + 1, 3)
+            place_feats(g + 3)

@@ -26,6 +26,8 @@ N_GROUPS = N_CHUNKS * GROUPS_PER_CHUNK
 CHUNKS_AHEAD = 3
 EDGE_TERM_AHEAD = 5
 
+N_TILES = N_GROUPS * TILES_PER_GROUP
+SUMS1_BANKS = 3
 RUN = 4
 
 FLOPS = 2 * E * ((NODE + 1) * MID + MID * OUT)
@@ -50,13 +52,14 @@ def tile_edgenetwork_kernel(
     def by_chunk(rows):
         return rows.rearrange("(q c i) f -> q c i f", c=P, i=TILES_PER_CHUNK)
 
-    hidden_inputs = (
+    node_inputs = (
+        (by_chunk(dst_node_feat), 0, 0, F),
         (by_chunk(dst_node_hidden), 0, F, 2 * F),
         (by_chunk(dst_node_hidden), 2 * F, 3 * F, F),
+        (by_chunk(src_node_feat), 0, F + H, F),
         (by_chunk(src_node_hidden), 0, 2 * F + H, 2 * F),
         (by_chunk(src_node_hidden), 2 * F, 4 * F + H, F),
     )
-    feat_inputs = (by_chunk(dst_node_feat), by_chunk(src_node_feat))
     out_by_chunk = by_chunk(out)
 
     with ExitStack() as stack:
@@ -67,28 +70,13 @@ def tile_edgenetwork_kernel(
 
         x_chunks = {}
 
-        feat_chunks = {}
-
         def load_chunk(q):
             x_sb = work.tile([P, TILES_PER_CHUNK, NODE], BF16, tag="x", bufs=CHUNKS_AHEAD + 1, name="x_sb")
-            for rows, first_in, first_x, width in hidden_inputs:
+            for rows, first_in, first_x, width in node_inputs:
                 nc.sync.dma_start(
                     out=x_sb[:, :, first_x : first_x + width], in_=rows[q][:, :, first_in : first_in + width]
                 )
-            feats = work.tile([P, 2, TILES_PER_CHUNK, F], BF16, tag="feats", bufs=CHUNKS_AHEAD + 1, name="feats")
-            for side, rows in enumerate(feat_inputs):
-                nc.sync.dma_start(out=feats[:, side, :, :], in_=rows[q])
             x_chunks[q] = x_sb
-            feat_chunks[q] = feats
-
-        def place_feats(g):
-            if not 0 <= g < N_GROUPS or g % GROUPS_PER_CHUNK != 0:
-                return
-            q = g // GROUPS_PER_CHUNK
-            nc.vector.tensor_copy(
-                out=x_chunks[q][:].rearrange("p i (side k) -> p side i k", side=2)[:, :, :, 0:F],
-                in_=feat_chunks[q][:],
-            )
 
         w1_rows = const.tile([P, PACK, NODE + 1], BF16)
         nc.sync.dma_start(out=w1_rows[:], in_=W1.rearrange("(j t) k -> j t k", t=PACK))
@@ -100,8 +88,8 @@ def tile_edgenetwork_kernel(
         )
         b1_bf = const.tile([P, PACK], BF16)
         nc.scalar.dma_start(out=b1_bf[:], in_=b1.rearrange("(p t) -> p t", t=PACK))
-        b2_bf = const.tile([P, OUT], BF16)
-        nc.scalar.dma_start(out=b2_bf[:], in_=b2.partition_broadcast(P))
+        b2_bf = const.tile([P, 1], BF16)
+        nc.scalar.dma_start(out=b2_bf[:], in_=b2.rearrange("(p o) -> p o", o=1))
         load_chunk(1)
 
         w2_codes = const.tile([P, OUT * PACK], U8, align_bytes=64)
@@ -129,9 +117,8 @@ def tile_edgenetwork_kernel(
         nc.vector.tensor_copy(out=w1_edge[:], in_=w1_rows[:, :, NODE])
         b1_f32 = const.tile([P, PACK], F32)
         nc.vector.tensor_copy(out=b1_f32[:], in_=b1_bf[:])
-        b2_f32 = const.tile([P, OUT], F32)
+        b2_f32 = const.tile([P, 1], F32)
         nc.vector.tensor_copy(out=b2_f32[:], in_=b2_bf[:])
-        place_feats(0)
 
         def transpose_rows(row_tiles):
             banks = []
@@ -194,7 +181,7 @@ def tile_edgenetwork_kernel(
                 return
             q = g // GROUPS_PER_CHUNK
             edge_all = work.tile([P, TILES_PER_CHUNK, P], BF16, tag="edge_all", name="edge_all")
-            nc.scalar.copy(out=edge_all[:], in_=spreads[q][:])
+            nc.vector.tensor_copy(out=edge_all[:], in_=spreads[q][:])
             edge_term = work.tile([P, PACK, TILES_PER_CHUNK, P], F32, tag="edge_term", bufs=3, name="edge_term")
             for t in range(PACK):
                 nc.gpsimd.tensor_scalar(
@@ -241,10 +228,11 @@ def tile_edgenetwork_kernel(
             x_scales[g] = work.tile([P, TILES_PER_GROUP * P], U8, tag="x_scales", align_bytes=64, name="x_scales")
             quantise(x_grouped[g][:], x_codes[g][:], x_scales[g][:])
 
-        def layer1(g, j):
-            if not in_range(g):
+        def layer1(n):
+            if not 0 <= n < N_TILES:
                 return
-            sums = psum.tile([P, PACK, P], F32, tag="sums1", bufs=4, name="sums")
+            g, j = divmod(n, TILES_PER_GROUP)
+            sums = psum.tile([P, PACK, P], F32, tag="sums1", bufs=SUMS1_BANKS, name="sums1_tile")
             cols = slice(P * j, P * (j + 1))
             for t in range(PACK):
                 block = slice(P * t, P * (t + 1))
@@ -257,19 +245,20 @@ def tile_edgenetwork_kernel(
                     start=True,
                     stop=True,
                 )
-            sums1[(g, j)] = sums
+            sums1[n] = sums
 
-        def hidden(g, j):
-            if not in_range(g):
+        def hidden(n):
+            if not 0 <= n < N_TILES:
                 return
-            q, half = divmod(g, GROUPS_PER_CHUNK)
+            g, j = divmod(n, TILES_PER_GROUP)
+            q, i = divmod(n, TILES_PER_CHUNK)
             if j == 0:
                 h_grouped[g] = work.tile([P, TILES_PER_GROUP, P * PACK], BF16, tag="h", bufs=3, align_bytes=64, name="h")
             pre = work.tile([P, PACK, P], BF16, tag="pre", bufs=3, name="pre")
             nc.vector.tensor_tensor(
                 out=pre[:],
-                in0=sums1[(g, j)][:],
-                in1=edge_terms[q][:, :, TILES_PER_GROUP * half + j, :],
+                in0=sums1[n][:],
+                in1=edge_terms[q][:, :, i, :],
                 op=ALU.add,
             )
             nc.scalar.activation(
@@ -288,40 +277,41 @@ def tile_edgenetwork_kernel(
         def layer2(g):
             if not in_range(g):
                 return
-            sums = psum.tile([P, TILES_PER_GROUP, OUT], F32, tag="sums2", name="sums")
-            for j in range(TILES_PER_GROUP):
-                cols = slice(P * j, P * (j + 1))
-                nc.tensor.matmul_mx(
-                    out=sums[:, j, :],
-                    lhsT=h_codes[g][:, cols].bitcast(FP8X4),
-                    lhsT_scale=h_scales[g][:, cols],
-                    rhs=w2_codes[:].bitcast(FP8X4),
-                    rhs_scale=w2_scales[:],
-                    start=True,
-                    stop=True,
-                )
+            sums = psum.tile([P, TILES_PER_GROUP * P], F32, tag="sums2", name="sums2_tile")
+            nc.tensor.matmul_mx(
+                out=sums[:],
+                lhsT=w2_codes[:].bitcast(FP8X4),
+                lhsT_scale=w2_scales[:],
+                rhs=h_codes[g][:].bitcast(FP8X4),
+                rhs_scale=h_scales[g][:],
+                start=True,
+                stop=True,
+            )
             sums2[g] = sums
 
-        biased_sums = {}
+        out_rows = {}
+        out_banks = {}
 
-        def add_b2(g):
+        def tanh(g):
             if not in_range(g):
                 return
-            biased = work.tile([P, TILES_PER_GROUP, OUT], F32, tag="biased", name="biased")
-            nc.vector.tensor_tensor(
-                out=biased[:],
-                in0=sums2[g][:],
-                in1=b2_f32[:].unsqueeze(1).to_broadcast([P, TILES_PER_GROUP, OUT]),
-                op=ALU.add,
-            )
-            biased_sums[g] = biased
+            out_rows[g] = work.tile([P, TILES_PER_GROUP * P], F32, tag="out_rows", name="out_rows")
+            nc.scalar.activation(out=out_rows[g][:], in_=sums2[g][:], func=ACT.Tanh, bias=b2_f32[:, 0:1])
 
-        def tanh_and_store(g):
+        def transpose_out(g):
+            if not in_range(g):
+                return
+            bank = psum.tile([P, TILES_PER_GROUP, OUT], F32, tag="out_bank", name="out_bank")
+            for j in range(TILES_PER_GROUP):
+                nc.tensor.transpose(bank[:, j, :], out_rows[g][:, P * j : P * (j + 1)], ident_f32[:])
+            out_banks[g] = bank
+
+        def store(g):
             if not in_range(g):
                 return
             q, half = divmod(g, GROUPS_PER_CHUNK)
             result = work.tile([P, TILES_PER_GROUP, OUT], F32, tag="result", bufs=3, name="result")
-            nc.scalar.activation(out=result[:], in_=biased_sums[g][:], func=ACT.Tanh)
+            nc.scalar.copy(out=result[:], in_=out_banks[g][:])
             first = TILES_PER_GROUP * half
             nc.sync.dma_start(out=out_by_chunk[q][:, first : first + TILES_PER_GROUP, :], in_=result[:])
 
@@ -329,22 +319,23 @@ def tile_edgenetwork_kernel(
             spread_edge(g + EDGE_TERM_AHEAD)
             prepare_edge_term(g + EDGE_TERM_AHEAD)
         for g in range(-2, N_GROUPS + 2):
+            first_tile = TILES_PER_GROUP * g
             transpose_x(g + 2)
             spread_edge(g + EDGE_TERM_AHEAD)
-            hidden(g, 0)
+            hidden(first_tile)
+            layer1(first_tile + SUMS1_BANKS)
             copy_out_x(g + 2, 0)
             quantise_x(g + 1)
-            layer1(g + 1, 0)
-            hidden(g, 1)
+            hidden(first_tile + 1)
+            layer1(first_tile + 1 + SUMS1_BANKS)
             copy_out_x(g + 2, 1)
             prepare_edge_term(g + EDGE_TERM_AHEAD)
-            layer1(g + 1, 1)
-            add_b2(g - 2)
-            hidden(g, 2)
-            tanh_and_store(g - 2)
-            layer1(g + 1, 2)
+            transpose_out(g - 2)
+            hidden(first_tile + 2)
+            layer1(first_tile + 2 + SUMS1_BANKS)
+            store(g - 2)
             quantise_h(g - 1)
             layer2(g - 1)
-            hidden(g, 3)
-            layer1(g + 1, 3)
-            place_feats(g + 3)
+            hidden(first_tile + 3)
+            layer1(first_tile + 3 + SUMS1_BANKS)
+            tanh(g - 1)

from contextlib import ExitStack

import concourse.mybir as mybir
from concourse.masks import make_identity

F32 = mybir.dt.float32
BF16 = mybir.dt.bfloat16
U32 = mybir.dt.uint32
U8 = mybir.dt.uint8
I32 = mybir.dt.int32
FP8X4 = mybir.dt.float8_e4m3fn_x4
ALU = mybir.AluOpType
ACT = mybir.ActivationFunctionType

P = 128
PACK = 4
E, F, H, MID, OUT = 16384, 64, 192, 512, 128
NODE = 2 * (F + H)
NODE_WORDS = NODE // 2

TILES_PER_GROUP = 4
TILES_PER_CHUNK = 8
GROUPS_PER_CHUNK = TILES_PER_CHUNK // TILES_PER_GROUP
N_CHUNKS = E // (P * TILES_PER_CHUNK)
N_GROUPS = N_CHUNKS * GROUPS_PER_CHUNK
CHUNKS_AHEAD = 3
EDGE_TERM_AHEAD = 5

N_TILES = N_GROUPS * TILES_PER_GROUP
SUMS1_BANKS = 3
RUN = 4

FLOPS = 2 * E * ((NODE + 1) * MID + MID * OUT)


def tile_edgenetwork_kernel(
    tc,
    dst_node_feat,
    dst_node_hidden,
    src_node_feat,
    src_node_hidden,
    edge_feat,
    W1,
    b1,
    W2_words,
    W2_scales,
    b2,
    out,
):
    nc = tc.nc

    def by_chunk(rows):
        return rows.rearrange("(q c i) f -> q c i f", c=P, i=TILES_PER_CHUNK)

    node_inputs = (
        (by_chunk(dst_node_feat), 0, 0, F),
        (by_chunk(dst_node_hidden), 0, F, 2 * F),
        (by_chunk(dst_node_hidden), 2 * F, 3 * F, F),
        (by_chunk(src_node_feat), 0, F + H, F),
        (by_chunk(src_node_hidden), 0, 2 * F + H, 2 * F),
        (by_chunk(src_node_hidden), 2 * F, 4 * F + H, F),
    )
    out_by_chunk = by_chunk(out)

    with ExitStack() as stack:
        const = stack.enter_context(tc.tile_pool(name="const", bufs=1))
        work = stack.enter_context(tc.tile_pool(name="work", bufs=2))
        psum = stack.enter_context(tc.psum_pool(name="psum", bufs=1))
        stack.enter_context(tc.manual_schedule())

        x_chunks = {}

        def load_chunk(q):
            x_sb = work.tile([P, TILES_PER_CHUNK, NODE], BF16, tag="x", bufs=CHUNKS_AHEAD + 1, name="x_sb")
            for rows, first_in, first_x, width in node_inputs:
                nc.sync.dma_start(
                    out=x_sb[:, :, first_x : first_x + width], in_=rows[q][:, :, first_in : first_in + width]
                )
            x_chunks[q] = x_sb

        w1_rows = const.tile([P, PACK, NODE + 1], BF16)
        nc.sync.dma_start(out=w1_rows[:], in_=W1.rearrange("(j t) k -> j t k", t=PACK))
        load_chunk(0)
        edge_cols = const.tile([P, N_CHUNKS * TILES_PER_CHUNK], BF16)
        nc.scalar.dma_start(
            out=edge_cols[:].rearrange("c (q i) -> c q i", i=TILES_PER_CHUNK),
            in_=edge_feat.rearrange("(q c i) -> c q i", c=P, i=TILES_PER_CHUNK),
        )
        b1_bf = const.tile([P, PACK], BF16)
        nc.scalar.dma_start(out=b1_bf[:], in_=b1.rearrange("(p t) -> p t", t=PACK))
        b2_bf = const.tile([P, 1], BF16)
        nc.scalar.dma_start(out=b2_bf[:], in_=b2.rearrange("(p o) -> p o", o=1))
        load_chunk(1)

        w2_codes = const.tile([P, OUT * PACK], U8, align_bytes=64)
        nc.sync.dma_start(
            out=w2_codes[:].bitcast(I32),
            in_=W2_words.rearrange("g p n t -> (g p) (n t)").bitcast(I32),
        )
        w2_scales = const.tile([P, OUT], U8, align_bytes=64)
        nc.vector.memset(w2_scales[:].bitcast(I32), 0)
        for quadrant in range(4):
            nc.sync.dma_start(
                out=w2_scales[32 * quadrant : 32 * quadrant + 4, :].bitcast(I32),
                in_=W2_scales[0, 4 * quadrant : 4 * quadrant + 4, :].bitcast(I32),
            )
        load_chunk(2)

        ident_f32 = const.tile([P, P], F32)
        make_identity(nc, ident_f32[:])
        ident_bf = const.tile([P, P], BF16)
        make_identity(nc, ident_bf[:])

        w1_nodes = const.tile([P, PACK, NODE], BF16)
        nc.vector.tensor_copy(out=w1_nodes[:], in_=w1_rows[:, :, 0:NODE])
        w1_edge = const.tile([P, PACK], F32)
        nc.vector.tensor_copy(out=w1_edge[:], in_=w1_rows[:, :, NODE])
        b1_f32 = const.tile([P, PACK], F32)
        nc.vector.tensor_copy(out=b1_f32[:], in_=b1_bf[:])
        b2_f32 = const.tile([P, 1], F32)
        nc.vector.tensor_copy(out=b2_f32[:], in_=b2_bf[:])

        def transpose_rows(row_tiles):
            banks = []
            for pair in range(2):
                xt = psum.tile([P, 4, P], F32, tag="xt", bufs=2, name="xt")
                for i in range(2):
                    words = row_tiles[2 * pair + i].bitcast(F32)
                    for u in range(2):
                        nc.tensor.transpose(xt[:, 2 * i + u, :], words[:, P * u : P * (u + 1)], ident_f32[:])
                banks.append(xt)
            return banks

        def new_grouped():
            return work.tile([P, TILES_PER_GROUP * P * PACK], BF16, tag="grouped", align_bytes=64, name="grouped")

        def copy_out(banks, grouped, pair):
            grouped_words = grouped[:].bitcast(F32)
            nc.scalar.copy(
                out=grouped_words[:, 512 * pair : 512 * (pair + 1)].rearrange("p (i c u) -> p i c u", i=2, u=2),
                in_=banks[pair][:].rearrange("p (i u) c -> p i c u", u=2),
            )

        def quantise(grouped, codes, scales):
            nc.vector.quantize_mx(out=codes.bitcast(FP8X4), scales=scales, in_=grouped)

        w1_codes = const.tile([P, PACK * P], U32, align_bytes=64)
        w1_scales = const.tile([P, PACK * P], U8, align_bytes=64)
        w1_banks = transpose_rows([w1_nodes[:, t, :] for t in range(PACK)])
        w1_grouped = new_grouped()
        copy_out(w1_banks, w1_grouped, 0)
        copy_out(w1_banks, w1_grouped, 1)
        quantise(w1_grouped[:], w1_codes[:], w1_scales[:])

        def in_range(g):
            return 0 <= g < N_GROUPS

        edge_terms = {}

        spreads = {}

        def spread_edge(g):
            if not in_range(g):
                return
            q, half = divmod(g, GROUPS_PER_CHUNK)
            if half == 0:
                spreads[q] = psum.tile([P, TILES_PER_CHUNK, P], BF16, tag="spread", name="spread")
            for j in range(TILES_PER_GROUP):
                i = TILES_PER_GROUP * half + j
                m = TILES_PER_CHUNK * q + i
                nc.tensor.matmul(
                    out=spreads[q][:, i, :],
                    lhsT=edge_cols[:, m : m + 1].to_broadcast([P, P]),
                    rhs=ident_bf[:],
                    start=True,
                    stop=True,
                )

        def prepare_edge_term(g):
            if not in_range(g) or g % GROUPS_PER_CHUNK != GROUPS_PER_CHUNK - 1:
                return
            q = g // GROUPS_PER_CHUNK
            edge_all = work.tile([P, TILES_PER_CHUNK, P], BF16, tag="edge_all", name="edge_all")
            nc.vector.tensor_copy(out=edge_all[:], in_=spreads[q][:])
            edge_term = work.tile([P, PACK, TILES_PER_CHUNK, P], F32, tag="edge_term", bufs=3, name="edge_term")
            for t in range(PACK):
                nc.gpsimd.tensor_scalar(
                    out=edge_term[:, t, :, :],
                    in0=edge_all[:],
                    scalar1=w1_edge[:, t : t + 1],
                    scalar2=b1_f32[:, t : t + 1],
                    op0=ALU.mult,
                    op1=ALU.add,
                )
            edge_terms[q] = edge_term

        x_grouped = {}
        x_codes = {}
        x_scales = {}
        sums1 = {}
        h_grouped = {}
        h_codes = {}
        h_scales = {}
        sums2 = {}

        x_banks = {}

        def transpose_x(g):
            if not in_range(g):
                return
            q, half = divmod(g, GROUPS_PER_CHUNK)
            if half == 0 and q + CHUNKS_AHEAD < N_CHUNKS:
                load_chunk(q + CHUNKS_AHEAD)
            x_sb = x_chunks[q]
            x_banks[g] = transpose_rows([x_sb[:, TILES_PER_GROUP * half + j, :] for j in range(TILES_PER_GROUP)])

        def copy_out_x(g, pair):
            if not in_range(g):
                return
            if pair == 0:
                x_grouped[g] = new_grouped()
            copy_out(x_banks[g], x_grouped[g], pair)

        def quantise_x(g):
            if not in_range(g):
                return
            x_codes[g] = work.tile([P, TILES_PER_GROUP * P], U32, tag="x_codes", align_bytes=64, name="x_codes")
            x_scales[g] = work.tile([P, TILES_PER_GROUP * P], U8, tag="x_scales", align_bytes=64, name="x_scales")
            quantise(x_grouped[g][:], x_codes[g][:], x_scales[g][:])

        def layer1(n):
            if not 0 <= n < N_TILES:
                return
            g, j = divmod(n, TILES_PER_GROUP)
            sums = psum.tile([P, PACK, P], F32, tag="sums1", bufs=SUMS1_BANKS, name="sums1_tile")
            cols = slice(P * j, P * (j + 1))
            for t in range(PACK):
                block = slice(P * t, P * (t + 1))
                nc.tensor.matmul_mx(
                    out=sums[:, t, :],
                    lhsT=w1_codes[:, block].bitcast(FP8X4),
                    lhsT_scale=w1_scales[:, block],
                    rhs=x_codes[g][:, cols].bitcast(FP8X4),
                    rhs_scale=x_scales[g][:, cols],
                    start=True,
                    stop=True,
                )
            sums1[n] = sums

        def hidden(n):
            if not 0 <= n < N_TILES:
                return
            g, j = divmod(n, TILES_PER_GROUP)
            q, i = divmod(n, TILES_PER_CHUNK)
            if j == 0:
                h_grouped[g] = work.tile([P, TILES_PER_GROUP, P * PACK], BF16, tag="h", bufs=3, align_bytes=64, name="h")
            pre = work.tile([P, PACK, P], BF16, tag="pre", bufs=3, name="pre")
            nc.vector.tensor_tensor(
                out=pre[:],
                in0=sums1[n][:],
                in1=edge_terms[q][:, :, i, :],
                op=ALU.add,
            )
            nc.scalar.activation(
                out=h_grouped[g][:, j, :].rearrange("p (b i t) -> p b t i", i=RUN, t=PACK),
                in_=pre[:].rearrange("p t (b i) -> p b t i", i=RUN),
                func=ACT.Relu,
            )

        def quantise_h(g):
            if not in_range(g):
                return
            h_codes[g] = work.tile([P, TILES_PER_GROUP * P], U32, tag="h_codes", align_bytes=64, name="h_codes")
            h_scales[g] = work.tile([P, TILES_PER_GROUP * P], U8, tag="h_scales", align_bytes=64, name="h_scales")
            quantise(h_grouped[g][:].rearrange("p j w -> p (j w)"), h_codes[g][:], h_scales[g][:])

        def layer2(g):
            if not in_range(g):
                return
            sums = psum.tile([P, TILES_PER_GROUP * P], F32, tag="sums2", name="sums2_tile")
            nc.tensor.matmul_mx(
                out=sums[:],
                lhsT=w2_codes[:].bitcast(FP8X4),
                lhsT_scale=w2_scales[:],
                rhs=h_codes[g][:].bitcast(FP8X4),
                rhs_scale=h_scales[g][:],
                start=True,
                stop=True,
            )
            sums2[g] = sums

        out_rows = {}
        out_banks = {}

        def tanh(g):
            if not in_range(g):
                return
            out_rows[g] = work.tile([P, TILES_PER_GROUP * P], F32, tag="out_rows", name="out_rows")
            nc.scalar.activation(out=out_rows[g][:], in_=sums2[g][:], func=ACT.Tanh, bias=b2_f32[:, 0:1])

        def transpose_out(g):
            if not in_range(g):
                return
            bank = psum.tile([P, TILES_PER_GROUP, OUT], F32, tag="out_bank", name="out_bank")
            for j in range(TILES_PER_GROUP):
                nc.tensor.transpose(bank[:, j, :], out_rows[g][:, P * j : P * (j + 1)], ident_f32[:])
            out_banks[g] = bank

        def store(g):
            if not in_range(g):
                return
            q, half = divmod(g, GROUPS_PER_CHUNK)
            result = work.tile([P, TILES_PER_GROUP, OUT], F32, tag="result", bufs=3, name="result")
            nc.scalar.copy(out=result[:], in_=out_banks[g][:])
            first = TILES_PER_GROUP * half
            nc.sync.dma_start(out=out_by_chunk[q][:, first : first + TILES_PER_GROUP, :], in_=result[:])

        for g in range(-2 - EDGE_TERM_AHEAD, -2):
            spread_edge(g + EDGE_TERM_AHEAD)
            prepare_edge_term(g + EDGE_TERM_AHEAD)
        for g in range(-2, N_GROUPS + 2):
            first_tile = TILES_PER_GROUP * g
            transpose_x(g + 2)
            spread_edge(g + EDGE_TERM_AHEAD)
            hidden(first_tile)
            layer1(first_tile + SUMS1_BANKS)
            copy_out_x(g + 2, 0)
            quantise_x(g + 1)
            hidden(first_tile + 1)
            layer1(first_tile + 1 + SUMS1_BANKS)
            copy_out_x(g + 2, 1)
            prepare_edge_term(g + EDGE_TERM_AHEAD)
            transpose_out(g - 2)
            hidden(first_tile + 2)
            layer1(first_tile + 2 + SUMS1_BANKS)
            store(g - 2)
            quantise_h(g - 1)
            layer2(g - 1)
            hidden(first_tile + 3)
            layer1(first_tile + 3 + SUMS1_BANKS)
            tanh(g - 1)
